import numpy as np
import ml_dtypes


def mxq(x, axis, fmt="e4m3"):
    dtype, down = {"e4m3": (ml_dtypes.float8_e4m3fn, 7), "e5m2": (ml_dtypes.float8_e5m2, 14)}[fmt]
    v = np.moveaxis(np.asarray(x, np.float32).astype(ml_dtypes.bfloat16).astype(np.float64), axis, -1)
    blocks = v.reshape(v.shape[:-1] + (-1, 32))
    amax = np.abs(blocks).max(-1, keepdims=True)
    byte = np.maximum(np.where(amax > 0, np.frexp(amax)[1] - 1 + 127, 0) - down, 1)
    scale = np.exp2(byte - 127.0)
    codes = (blocks / scale).astype(np.float32).astype(dtype).astype(np.float64)
    return np.moveaxis((codes * scale).reshape(v.shape), -1, axis)


WIDE = False


def mx_kscale(k):
    if not WIDE:
        return np.ones(k)
    levels = np.array([10, -10, 5, -5, 0])
    a = np.random.permutation(np.resize(levels, k // 512 * 4)).reshape(k // 512, 4)
    idx = np.arange(k)
    return np.exp2(a[idx // 512, idx % 128 // 32])


BF16 = ml_dtypes.bfloat16


def bf(x):
    return np.asarray(x, np.float32).astype(BF16)


def f64(x):
    return np.asarray(x).astype(np.float64)


B, H = 4096, 512


def sigmoid(v):
    return 1.0 / (1.0 + np.exp(-v))


def setup_inputs():
    s = mx_kscale(H)
    w = lambda: bf(np.random.standard_normal((H, H)) * 0.7 / np.sqrt(H) / s[None, :])
    b = lambda: bf(np.random.standard_normal(H) * 0.5)
    return {"inputs": bf(np.random.standard_normal((B, H)) * s),
            "short_term_memory": bf(np.random.standard_normal((B, H)) * s),
            "Wf": w(), "b_f": b(), "Wi": w(), "b_i": b(), "Wg": w(), "b_g": b(), "Wo": w(), "b_o": b()}


def reference(inputs, short_term_memory, Wf, b_f, Wi, b_i, Wg, b_g, Wo, b_o):
    z = f64(inputs) + f64(short_term_memory)
    zq = mxq(z, 1, "e4m3")
    c = sigmoid((zq @ mxq(f64(Wf), 1, "e4m3").T) + f64(b_f))
    c = c + sigmoid((zq @ mxq(f64(Wi), 1, "e4m3").T) + f64(b_i)) * np.tanh((zq @ mxq(f64(Wg), 1, "e4m3").T) + f64(b_g))
    h = np.tanh(c) * sigmoid((zq @ mxq(f64(Wo), 1, "e4m3").T) + f64(b_o))
    return np.stack((c, h))

@@ -1,0 +1,277 @@
+from contextlib import ExitStack
+
+import concourse.mybir as mybir
+from concourse.masks import make_identity
+
+F32 = mybir.dt.float32
+BF16 = mybir.dt.bfloat16
+U32 = mybir.dt.uint32
+U8 = mybir.dt.uint8
+FP8X4 = mybir.dt.float8_e4m3fn_x4
+ACT = mybir.ActivationFunctionType
+ALU = mybir.AluOpType
+
+B = 4096
+H = 512
+P = 128
+GATES = 4
+ROUND = 512
+CHUNKS = H // P
+BLOCKS = ROUND // P
+STEPS = (B // ROUND) * CHUNKS
+HALVES = 2
+UNIT = 2
+UNIT_COLS = UNIT * P
+PAIRS = BLOCKS // UNIT
+GATE_UNITS = GATES // UNIT
+Z_UNITS = B // (UNIT * P)
+LEAD = 6
+LOADS_AHEAD = 4
+
+FLOPS = 2 * B * H * GATES * H
+
+
+def tile_lstmcell_pa_t_kernel(
+    tc, inputs, short_term_memory, Wf, b_f, Wi, b_i, Wg, b_g, Wo, b_o, out
+):
+    nc = tc.nc
+    weights = [Wi, Wg, Wf, Wo]
+    biases = [b_i, b_g, b_f, b_o]
+    functions = [ACT.Sigmoid, ACT.Tanh, ACT.Sigmoid, ACT.Sigmoid]
+    gate_names = ["sig_i", "tanh_g", "sig_f", "sig_o"]
+    x_view = inputs.rearrange("(r p a t) k -> r a p t k", p=P, a=PAIRS, t=UNIT)
+    h_view = short_term_memory.rearrange("(r p a t) k -> r a p t k", p=P, a=PAIRS, t=UNIT)
+    out_view = out.rearrange("o (r p s) f -> o r p s f", p=P, s=BLOCKS)
+
+    with ExitStack() as ctx:
+        keep = ctx.enter_context(tc.tile_pool(name="keep", bufs=1))
+        loads = ctx.enter_context(tc.tile_pool(name="loads", bufs=LOADS_AHEAD))
+        prep = ctx.enter_context(tc.tile_pool(name="prep", bufs=3))
+        gate_pool = ctx.enter_context(tc.tile_pool(name="gates", bufs=4))
+        cell_pool = ctx.enter_context(tc.tile_pool(name="cells", bufs=3))
+        round_pool = ctx.enter_context(tc.tile_pool(name="rounds", bufs=2))
+        acc_pool = ctx.enter_context(tc.psum_pool(name="acc", bufs=GATES))
+        turn_pool = ctx.enter_context(tc.psum_pool(name="turned", bufs=2))
+        back_pool = ctx.enter_context(tc.psum_pool(name="back", bufs=1))
+
+        ident = keep.tile([P, P], F32, name="ident")
+        make_identity(nc, ident[:])
+
+        ctx.enter_context(tc.manual_schedule())
+
+        w_raw = keep.tile([P, CHUNKS, GATES, H], BF16, name="w_raw")
+        w_codes = keep.tile([P, CHUNKS, GATES, P], U32, name="w_codes", align_bytes=64)
+        w_scales = keep.tile([P, CHUNKS, GATES, P], U8, name="w_scales", align_bytes=64)
+        bias_rows = keep.tile([P, P], BF16, name="bias_rows")
+        bias_rows_f32 = keep.tile([P, P], F32, name="bias_rows_f32")
+        bias = keep.tile([P, GATES * CHUNKS], F32, name="bias")
+
+        x_raw = {}
+        h_raw = {}
+        z_sum = {}
+        z_turned = {}
+        z_grouped = {}
+        z_codes = {}
+        z_scales = {}
+        acc = {}
+        gate = {}
+        product = {}
+        cell_t = {}
+        cell_rows = {}
+        sig_o_rows = {}
+        tanh_c = {}
+        cell_round = {}
+        hidden_round = {}
+
+
+        def turn(source):
+            turned = turn_pool.tile([P, UNIT, HALVES, P], F32, name="turned")
+            for t in range(UNIT):
+                words = source[:, t, :].bitcast(F32)
+                for u in range(HALVES):
+                    nc.tensor.transpose(turned[:, t, u, :], words[:, u * P : (u + 1) * P], ident[:])
+            return turned
+
+        def group(turned):
+            grouped = prep.tile([P, UNIT * H], BF16, name="grouped", align_bytes=64)
+            nc.vector.tensor_copy(
+                out=grouped[:].bitcast(F32).rearrange("p (t c u) -> p t c u", t=UNIT, u=HALVES),
+                in_=turned[:].rearrange("p t u c -> p t c u"),
+            )
+            return grouped
+
+        def quantise(grouped, codes, scales):
+            nc.vector.quantize_mx(out=codes.bitcast(FP8X4), scales=scales, in_=grouped[:])
+
+
+        def load_weights(m):
+            for g in range(GATES):
+                nc.sync.dma_start(out=w_raw[:, m, g, :], in_=weights[g][m * P : (m + 1) * P, :])
+
+        def prepare_weights(m):
+            grouped = []
+            for v in range(GATE_UNITS):
+                grouped.append(group(turn(w_raw[:, m, v * UNIT : (v + 1) * UNIT, :])))
+            for v in range(GATE_UNITS):
+                gates_of_unit = slice(v * UNIT, (v + 1) * UNIT)
+                quantise(
+                    grouped[v],
+                    w_codes[:, m, gates_of_unit, :].rearrange("p g o -> p (g o)"),
+                    w_scales[:, m, gates_of_unit, :].rearrange("p g o -> p (g o)"),
+                )
+
+        def load_biases():
+            nc.vector.memset(bias_rows[:], 0.0)
+            for g in range(GATES):
+                nc.scalar.dma_start(
+                    out=bias_rows[g * CHUNKS : (g + 1) * CHUNKS, :],
+                    in_=biases[g].rearrange("(m c) -> m c", c=P),
+                )
+
+        def prepare_biases():
+            nc.vector.tensor_copy(out=bias_rows_f32[:], in_=bias_rows[:])
+            turned = turn_pool.tile([P, UNIT, HALVES, P], F32, name="turned")
+            nc.tensor.transpose(turned[:, 0, 0, :], bias_rows_f32[:], ident[:])
+            nc.vector.tensor_copy(out=bias[:], in_=turned[:, 0, 0, 0 : GATES * CHUNKS])
+
+
+        def load_unit(q):
+            r, a = divmod(q, PAIRS)
+            x_raw[q] = loads.tile([P, UNIT, H], BF16, name="x_raw")
+            nc.sync.dma_start(out=x_raw[q][:], in_=x_view[r, a])
+            h_raw[q] = loads.tile([P, UNIT, H], BF16, name="h_raw")
+            nc.sync.dma_start(out=h_raw[q][:], in_=h_view[r, a])
+
+        def add_z(q):
+            z_sum[q] = prep.tile([P, UNIT, H], BF16, name="z_sum")
+            nc.vector.tensor_tensor(out=z_sum[q][:], in0=x_raw[q][:], in1=h_raw[q][:], op=ALU.add)
+
+        def quantise_z(q):
+            r, a = divmod(q, PAIRS)
+            if a == 0:
+                z_codes[r] = prep.tile([P, ROUND], U32, name="z_codes", align_bytes=64)
+                z_scales[r] = prep.tile([P, ROUND], U8, name="z_scales", align_bytes=64)
+            columns = slice(a * UNIT_COLS, (a + 1) * UNIT_COLS)
+            quantise(z_grouped[q], z_codes[r][:, columns], z_scales[r][:, columns])
+
+
+        def multiply(n):
+            r, m = divmod(n, CHUNKS)
+            for g in range(GATES):
+                acc[n, g] = acc_pool.tile([P, ROUND], F32, name="acc")
+                nc.tensor.matmul_mx(
+                    out=acc[n, g][:],
+                    lhsT=w_codes[:, m, g, :].bitcast(FP8X4),
+                    lhsT_scale=w_scales[:, m, g, :],
+                    rhs=z_codes[r][:].bitcast(FP8X4),
+                    rhs_scale=z_scales[r][:],
+                    start=True,
+                    stop=True,
+                )
+
+        def activate(n):
+            m = n % CHUNKS
+            for g in range(GATES):
+                gate[n, g] = gate_pool.tile([P, ROUND], F32, name=gate_names[g])
+                column = g * CHUNKS + m
+                nc.scalar.activation(
+                    out=gate[n, g][:],
+                    in_=acc[n, g][:],
+                    func=functions[g],
+                    bias=bias[:, column : column + 1],
+                    scale=1.0,
+                )
+
+        def multiply_gates(n):
+            product[n] = cell_pool.tile([P, ROUND], F32, name="product")
+            nc.gpsimd.tensor_tensor(
+                out=product[n][:], in0=gate[n, 0][:], in1=gate[n, 1][:], op=ALU.mult
+            )
+
+        def add_cell(n):
+            cell_t[n] = cell_pool.tile([P, ROUND], F32, name="cell_t")
+            nc.vector.tensor_tensor(
+                out=cell_t[n][:], in0=gate[n, 2][:], in1=product[n][:], op=ALU.add
+            )
+
+        def turn_back(source, name):
+            rows = back_pool.tile([P, BLOCKS, P], F32, name=name)
+            for s in range(BLOCKS):
+                nc.tensor.transpose(rows[:, s, :], source[:, s * P : (s + 1) * P], ident[:])
+            return rows
+
+        def copy_cell(n):
+            r, m = divmod(n, CHUNKS)
+            if m == 0:
+                cell_round[r] = round_pool.tile([P, BLOCKS, H], F32, name="cell_round")
+            features = slice(m * P, (m + 1) * P)
+            nc.vector.tensor_copy(out=cell_round[r][:, :, features], in_=cell_rows[n][:])
+            if m == CHUNKS - 1:
+                nc.sync.dma_start(out=out_view[0, r], in_=cell_round[r][:])
+
+        def tanh_cell(n):
+            r, m = divmod(n, CHUNKS)
+            tanh_c[n] = cell_pool.tile([P, BLOCKS, P], F32, name="tanh_c")
+            nc.scalar.activation(
+                out=tanh_c[n][:], in_=cell_round[r][:, :, m * P : (m + 1) * P], func=ACT.Tanh
+            )
+
+        def hidden(n):
+            r, m = divmod(n, CHUNKS)
+            if m == 0:
+                hidden_round[r] = round_pool.tile([P, BLOCKS, H], F32, name="hidden_round")
+            nc.vector.tensor_tensor(
+                out=hidden_round[r][:, :, m * P : (m + 1) * P],
+                in0=tanh_c[n][:],
+                in1=sig_o_rows[n][:],
+                op=ALU.mult,
+            )
+            if m == CHUNKS - 1:
+                nc.sync.dma_start(out=out_view[1, r], in_=hidden_round[r][:])
+
+
+        load_biases()
+        load_weights(0)
+        load_unit(0)
+        load_unit(1)
+        load_weights(1)
+        load_unit(2)
+        load_weights(2)
+        load_unit(3)
+        load_weights(3)
+        prepare_weights(0)
+        prepare_biases()
+
+        for n in range(-LEAD, STEPS + 2):
+            started = 0 <= n - 1 < STEPS
+            finishing = 0 <= n - 2 < STEPS
+            q, odd = divmod(n + LEAD, 2)
+
+            if started:
+                add_cell(n - 1)
+                cell_rows[n - 1] = turn_back(cell_t[n - 1], "cell_rows")
+            if finishing:
+                sig_o_rows[n - 2] = turn_back(gate[n - 2, 3], "sig_o_rows")
+            if not odd and 0 <= q - 1 < Z_UNITS:
+                quantise_z(q - 1)
+            if not odd and q < Z_UNITS:
+                add_z(q)
+                z_turned[q] = turn(z_sum[q])
+                if q + LOADS_AHEAD < Z_UNITS:
+                    load_unit(q + LOADS_AHEAD)
+
+            if 0 <= n < STEPS:
+                activate(n)
+                multiply_gates(n)
+            if 0 <= n + 1 < STEPS:
+                multiply(n + 1)
+
+            if started:
+                copy_cell(n - 1)
+                tanh_cell(n - 1)
+            if finishing:
+                hidden(n - 2)
+            if odd and q < Z_UNITS:
+                z_grouped[q] = group(z_turned[q])
+            if 1 <= n + 2 < CHUNKS:
+                prepare_weights(n + 2)

@@ -25,8 +25,11 @@ UNIT_COLS = UNIT * P
 PAIRS = BLOCKS // UNIT
 GATE_UNITS = GATES // UNIT
 Z_UNITS = B // (UNIT * P)
+FIRST_UNITS = PAIRS
+FIRST_CHUNKS = 2
 LEAD = 6
 LOADS_AHEAD = 4
+LAST_LAG = 4
 
 FLOPS = 2 * B * H * GATES * H
 
@@ -47,12 +50,13 @@ def tile_lstmcell_pa_t_kernel(
         keep = ctx.enter_context(tc.tile_pool(name="keep", bufs=1))
         loads = ctx.enter_context(tc.tile_pool(name="loads", bufs=LOADS_AHEAD))
         prep = ctx.enter_context(tc.tile_pool(name="prep", bufs=3))
-        gate_pool = ctx.enter_context(tc.tile_pool(name="gates", bufs=4))
+        w_prep = ctx.enter_context(tc.tile_pool(name="w_prep", bufs=FIRST_CHUNKS * GATE_UNITS))
+        gate_pool = ctx.enter_context(tc.tile_pool(name="gates", bufs=LAST_LAG + 1))
         cell_pool = ctx.enter_context(tc.tile_pool(name="cells", bufs=3))
         round_pool = ctx.enter_context(tc.tile_pool(name="rounds", bufs=2))
         acc_pool = ctx.enter_context(tc.psum_pool(name="acc", bufs=GATES))
-        turn_pool = ctx.enter_context(tc.psum_pool(name="turned", bufs=2))
-        back_pool = ctx.enter_context(tc.psum_pool(name="back", bufs=1))
+        cell_bank = ctx.enter_context(tc.psum_pool(name="cell_bank", bufs=1))
+        turn_pool = ctx.enter_context(tc.psum_pool(name="turned", bufs=3))
 
         ident = keep.tile([P, P], F32, name="ident")
         make_identity(nc, ident[:])
@@ -65,7 +69,11 @@ def tile_lstmcell_pa_t_kernel(
         bias_rows = keep.tile([P, P], BF16, name="bias_rows")
         bias_rows_f32 = keep.tile([P, P], F32, name="bias_rows_f32")
         bias = keep.tile([P, GATES * CHUNKS], F32, name="bias")
+        zero = keep.tile([P, 1], F32, name="zero")
+        half = keep.tile([P, 1], F32, name="half")
 
+        w_turned = {}
+        w_grouped = {}
         x_raw = {}
         h_raw = {}
         z_sum = {}
@@ -85,16 +93,16 @@ def tile_lstmcell_pa_t_kernel(
 
 
         def turn(source):
-            turned = turn_pool.tile([P, UNIT, HALVES, P], F32, name="turned")
+            turned = turn_pool.tile([P, UNIT, HALVES, P], F32, name="unit_turned", tag="turned")
             for t in range(UNIT):
                 words = source[:, t, :].bitcast(F32)
                 for u in range(HALVES):
                     nc.tensor.transpose(turned[:, t, u, :], words[:, u * P : (u + 1) * P], ident[:])
             return turned
 
-        def group(turned):
-            grouped = prep.tile([P, UNIT * H], BF16, name="grouped", align_bytes=64)
-            nc.vector.tensor_copy(
+        def group(turned, pool, copy):
+            grouped = pool.tile([P, UNIT * H], BF16, name="grouped", align_bytes=64)
+            copy(
                 out=grouped[:].bitcast(F32).rearrange("p (t c u) -> p t c u", t=UNIT, u=HALVES),
                 in_=turned[:].rearrange("p t u c -> p t c u"),
             )
@@ -108,14 +116,19 @@ def tile_lstmcell_pa_t_kernel(
             for g in range(GATES):
                 nc.sync.dma_start(out=w_raw[:, m, g, :], in_=weights[g][m * P : (m + 1) * P, :])
 
-        def prepare_weights(m):
-            grouped = []
-            for v in range(GATE_UNITS):
-                grouped.append(group(turn(w_raw[:, m, v * UNIT : (v + 1) * UNIT, :])))
+        def turn_weights(m):
+            w_turned[m] = [
+                turn(w_raw[:, m, v * UNIT : (v + 1) * UNIT, :]) for v in range(GATE_UNITS)
+            ]
+
+        def group_weights(m, copy):
+            w_grouped[m] = [group(turned, w_prep, copy) for turned in w_turned[m]]
+
+        def quantise_weights(m):
             for v in range(GATE_UNITS):
                 gates_of_unit = slice(v * UNIT, (v + 1) * UNIT)
                 quantise(
-                    grouped[v],
+                    w_grouped[m][v],
                     w_codes[:, m, gates_of_unit, :].rearrange("p g o -> p (g o)"),
                     w_scales[:, m, gates_of_unit, :].rearrange("p g o -> p (g o)"),
                 )
@@ -128,12 +141,6 @@ def tile_lstmcell_pa_t_kernel(
                     in_=biases[g].rearrange("(m c) -> m c", c=P),
                 )
 
-        def prepare_biases():
-            nc.vector.tensor_copy(out=bias_rows_f32[:], in_=bias_rows[:])
-            turned = turn_pool.tile([P, UNIT, HALVES, P], F32, name="turned")
-            nc.tensor.transpose(turned[:, 0, 0, :], bias_rows_f32[:], ident[:])
-            nc.vector.tensor_copy(out=bias[:], in_=turned[:, 0, 0, 0 : GATES * CHUNKS])
-
 
         def load_unit(q):
             r, a = divmod(q, PAIRS)
@@ -145,6 +152,8 @@ def tile_lstmcell_pa_t_kernel(
         def add_z(q):
             z_sum[q] = prep.tile([P, UNIT, H], BF16, name="z_sum")
             nc.vector.tensor_tensor(out=z_sum[q][:], in0=x_raw[q][:], in1=h_raw[q][:], op=ALU.add)
+            if q + LOADS_AHEAD < Z_UNITS:
+                load_unit(q + LOADS_AHEAD)
 
         def quantise_z(q):
             r, a = divmod(q, PAIRS)
@@ -194,18 +203,25 @@ def tile_lstmcell_pa_t_kernel(
                 out=cell_t[n][:], in0=gate[n, 2][:], in1=product[n][:], op=ALU.add
             )
 
-        def turn_back(source, name):
-            rows = back_pool.tile([P, BLOCKS, P], F32, name=name)
+        def turn_back(rows, source):
             for s in range(BLOCKS):
                 nc.tensor.transpose(rows[:, s, :], source[:, s * P : (s + 1) * P], ident[:])
-            return rows
+
+        def turn_cell(n):
+            cell_rows[n] = cell_bank.tile([P, BLOCKS, P], F32, name="cell_rows")
+            turn_back(cell_rows[n], cell_t[n])
+
+        def turn_sig_o(n):
+            sig_o_rows[n] = turn_pool.tile([P, BLOCKS, P], F32, name="sig_o_rows", tag="turned")
+            turn_back(sig_o_rows[n], gate[n, 3])
 
         def copy_cell(n):
             r, m = divmod(n, CHUNKS)
             if m == 0:
                 cell_round[r] = round_pool.tile([P, BLOCKS, H], F32, name="cell_round")
-            features = slice(m * P, (m + 1) * P)
-            nc.vector.tensor_copy(out=cell_round[r][:, :, features], in_=cell_rows[n][:])
+            nc.vector.tensor_copy(
+                out=cell_round[r][:, :, m * P : (m + 1) * P], in_=cell_rows[n][:]
+            )
             if m == CHUNKS - 1:
                 nc.sync.dma_start(out=out_view[0, r], in_=cell_round[r][:])
 
@@ -231,47 +247,69 @@ def tile_lstmcell_pa_t_kernel(
 
 
         load_biases()
-        load_weights(0)
         load_unit(0)
         load_unit(1)
+        load_weights(0)
         load_weights(1)
         load_unit(2)
         load_weights(2)
         load_unit(3)
         load_weights(3)
-        prepare_weights(0)
-        prepare_biases()
 
-        for n in range(-LEAD, STEPS + 2):
-            started = 0 <= n - 1 < STEPS
-            finishing = 0 <= n - 2 < STEPS
+        nc.vector.memset(zero[:], 0.0)
+        nc.scalar.activation(out=half[:], in_=zero[:], func=ACT.Sigmoid)
+
+        for q in range(FIRST_UNITS):
+            add_z(q)
+            z_turned[q] = turn(z_sum[q])
+        nc.vector.tensor_copy(out=bias_rows_f32[:], in_=bias_rows[:])
+        bias_turned = cell_bank.tile([P, BLOCKS, P], F32, name="bias_turned", tag="cell_rows")
+        nc.tensor.transpose(bias_turned[:, 0, :], bias_rows_f32[:], ident[:])
+        for q in range(FIRST_UNITS):
+            z_grouped[q] = group(z_turned[q], prep, nc.vector.tensor_copy)
+        nc.vector.tensor_copy(out=bias[:], in_=bias_turned[:, 0, 0 : GATES * CHUNKS])
+        for m in range(FIRST_CHUNKS):
+            turn_weights(m)
+            group_weights(m, nc.scalar.copy)
+        for q in range(FIRST_UNITS):
+            quantise_z(q)
+        quantise_weights(0)
+        multiply(0)
+        quantise_weights(1)
+
+
+        for n in range(2 * FIRST_UNITS - LEAD, STEPS + LAST_LAG):
             q, odd = divmod(n + LEAD, 2)
 
-            if started:
+            if 0 <= n - 1 < STEPS:
                 add_cell(n - 1)
-                cell_rows[n - 1] = turn_back(cell_t[n - 1], "cell_rows")
-            if finishing:
-                sig_o_rows[n - 2] = turn_back(gate[n - 2, 3], "sig_o_rows")
-            if not odd and 0 <= q - 1 < Z_UNITS:
+            if not odd and FIRST_UNITS <= q - 1 < Z_UNITS:
                 quantise_z(q - 1)
             if not odd and q < Z_UNITS:
                 add_z(q)
-                z_turned[q] = turn(z_sum[q])
-                if q + LOADS_AHEAD < Z_UNITS:
-                    load_unit(q + LOADS_AHEAD)
+            if 0 <= n - 2 < STEPS:
+                copy_cell(n - 2)
+            if 0 <= n - LAST_LAG < STEPS:
+                hidden(n - LAST_LAG)
+            if odd and q < Z_UNITS:
+                z_grouped[q] = group(z_turned[q], prep, nc.vector.tensor_copy)
+            if FIRST_CHUNKS <= n + 2 < CHUNKS:
+                group_weights(n + 2, nc.vector.tensor_copy)
+                quantise_weights(n + 2)
 
             if 0 <= n < STEPS:
                 activate(n)
                 multiply_gates(n)
-            if 0 <= n + 1 < STEPS:
-                multiply(n + 1)
+            if 0 <= n - 3 < STEPS:
+                tanh_cell(n - 3)
 
-            if started:
-                copy_cell(n - 1)
-                tanh_cell(n - 1)
-            if finishing:
-                hidden(n - 2)
-            if odd and q < Z_UNITS:
-                z_grouped[q] = group(z_turned[q])
-            if 1 <= n + 2 < CHUNKS:
-                prepare_weights(n + 2)
+            if 1 <= n + 1 < STEPS:
+                multiply(n + 1)
+            if 0 <= n - 1 < STEPS:
+                turn_cell(n - 1)
+            if 0 <= n - 3 < STEPS:
+                turn_sig_o(n - 3)
+            if not odd and q < Z_UNITS:
+                z_turned[q] = turn(z_sum[q])
+            if FIRST_CHUNKS <= n + 3 < CHUNKS:
+                turn_weights(n + 3)

@@ -15,6 +15,10 @@ B = 4096
 H = 512
 P = 128
 GATES = 4
+I_GATE = 0
+G_GATE = 1
+F_GATE = 2
+O_GATE = 3
 ROUND = 512
 CHUNKS = H // P
 BLOCKS = ROUND // P
@@ -44,7 +48,7 @@ def tile_lstmcell_pa_t_kernel(
     gate_names = ["sig_i", "tanh_g", "sig_f", "sig_o"]
     x_view = inputs.rearrange("(r p a t) k -> r a p t k", p=P, a=PAIRS, t=UNIT)
     h_view = short_term_memory.rearrange("(r p a t) k -> r a p t k", p=P, a=PAIRS, t=UNIT)
-    out_view = out.rearrange("o (r p s) f -> o r p s f", p=P, s=BLOCKS)
+    out_view = out.rearrange("o (r p s) (m f) -> o r m p s f", p=P, s=BLOCKS, f=P)
 
     with ExitStack() as ctx:
         keep = ctx.enter_context(tc.tile_pool(name="keep", bufs=1))
@@ -53,7 +57,7 @@ def tile_lstmcell_pa_t_kernel(
         w_prep = ctx.enter_context(tc.tile_pool(name="w_prep", bufs=FIRST_CHUNKS * GATE_UNITS))
         gate_pool = ctx.enter_context(tc.tile_pool(name="gates", bufs=LAST_LAG + 1))
         cell_pool = ctx.enter_context(tc.tile_pool(name="cells", bufs=3))
-        round_pool = ctx.enter_context(tc.tile_pool(name="rounds", bufs=2))
+        result_pool = ctx.enter_context(tc.tile_pool(name="results", bufs=4))
         acc_pool = ctx.enter_context(tc.psum_pool(name="acc", bufs=GATES))
         cell_bank = ctx.enter_context(tc.psum_pool(name="cell_bank", bufs=1))
         turn_pool = ctx.enter_context(tc.psum_pool(name="turned", bufs=3))
@@ -87,9 +91,8 @@ def tile_lstmcell_pa_t_kernel(
         cell_t = {}
         cell_rows = {}
         sig_o_rows = {}
+        cell = {}
         tanh_c = {}
-        cell_round = {}
-        hidden_round = {}
 
 
         def turn(source):
@@ -178,29 +181,27 @@ def tile_lstmcell_pa_t_kernel(
                     stop=True,
                 )
 
-        def activate(n):
-            m = n % CHUNKS
-            for g in range(GATES):
-                gate[n, g] = gate_pool.tile([P, ROUND], F32, name=gate_names[g])
-                column = g * CHUNKS + m
-                nc.scalar.activation(
-                    out=gate[n, g][:],
-                    in_=acc[n, g][:],
-                    func=functions[g],
-                    bias=bias[:, column : column + 1],
-                    scale=1.0,
-                )
+        def activate(n, g):
+            gate[n, g] = gate_pool.tile([P, ROUND], F32, name=gate_names[g])
+            column = g * CHUNKS + n % CHUNKS
+            nc.scalar.activation(
+                out=gate[n, g][:],
+                in_=acc[n, g][:],
+                func=functions[g],
+                bias=bias[:, column : column + 1],
+                scale=1.0,
+            )
 
         def multiply_gates(n):
             product[n] = cell_pool.tile([P, ROUND], F32, name="product")
             nc.gpsimd.tensor_tensor(
-                out=product[n][:], in0=gate[n, 0][:], in1=gate[n, 1][:], op=ALU.mult
+                out=product[n][:], in0=gate[n, I_GATE][:], in1=gate[n, G_GATE][:], op=ALU.mult
             )
 
         def add_cell(n):
             cell_t[n] = cell_pool.tile([P, ROUND], F32, name="cell_t")
             nc.vector.tensor_tensor(
-                out=cell_t[n][:], in0=gate[n, 2][:], in1=product[n][:], op=ALU.add
+                out=cell_t[n][:], in0=gate[n, F_GATE][:], in1=product[n][:], op=ALU.add
             )
 
         def turn_back(rows, source):
@@ -213,37 +214,25 @@ def tile_lstmcell_pa_t_kernel(
 
         def turn_sig_o(n):
             sig_o_rows[n] = turn_pool.tile([P, BLOCKS, P], F32, name="sig_o_rows", tag="turned")
-            turn_back(sig_o_rows[n], gate[n, 3])
+            turn_back(sig_o_rows[n], gate[n, O_GATE])
 
         def copy_cell(n):
             r, m = divmod(n, CHUNKS)
-            if m == 0:
-                cell_round[r] = round_pool.tile([P, BLOCKS, H], F32, name="cell_round")
-            nc.vector.tensor_copy(
-                out=cell_round[r][:, :, m * P : (m + 1) * P], in_=cell_rows[n][:]
-            )
-            if m == CHUNKS - 1:
-                nc.sync.dma_start(out=out_view[0, r], in_=cell_round[r][:])
+            cell[n] = result_pool.tile([P, BLOCKS, P], F32, name="cell")
+            nc.vector.tensor_copy(out=cell[n][:], in_=cell_rows[n][:])
+            nc.sync.dma_start(out=out_view[0, r, m], in_=cell[n][:])
 
         def tanh_cell(n):
-            r, m = divmod(n, CHUNKS)
             tanh_c[n] = cell_pool.tile([P, BLOCKS, P], F32, name="tanh_c")
-            nc.scalar.activation(
-                out=tanh_c[n][:], in_=cell_round[r][:, :, m * P : (m + 1) * P], func=ACT.Tanh
-            )
+            nc.scalar.activation(out=tanh_c[n][:], in_=cell[n][:], func=ACT.Tanh)
 
         def hidden(n):
             r, m = divmod(n, CHUNKS)
-            if m == 0:
-                hidden_round[r] = round_pool.tile([P, BLOCKS, H], F32, name="hidden_round")
+            hidden_rows = result_pool.tile([P, BLOCKS, P], F32, name="hidden_rows")
             nc.vector.tensor_tensor(
-                out=hidden_round[r][:, :, m * P : (m + 1) * P],
-                in0=tanh_c[n][:],
-                in1=sig_o_rows[n][:],
-                op=ALU.mult,
+                out=hidden_rows[:], in0=tanh_c[n][:], in1=sig_o_rows[n][:], op=ALU.mult
             )
-            if m == CHUNKS - 1:
-                nc.sync.dma_start(out=out_view[1, r], in_=hidden_round[r][:])
+            nc.sync.dma_start(out=out_view[1, r, m], in_=hidden_rows[:])
 
 
         load_biases()
@@ -298,10 +287,14 @@ def tile_lstmcell_pa_t_kernel(
                 quantise_weights(n + 2)
 
             if 0 <= n < STEPS:
-                activate(n)
+                activate(n, I_GATE)
+                activate(n, G_GATE)
                 multiply_gates(n)
+                activate(n, F_GATE)
             if 0 <= n - 3 < STEPS:
                 tanh_cell(n - 3)
+            if 0 <= n < STEPS:
+                activate(n, O_GATE)
 
             if 1 <= n + 1 < STEPS:
                 multiply(n + 1)

@@ -291,10 +291,9 @@ def tile_lstmcell_pa_t_kernel(
                 activate(n, G_GATE)
                 multiply_gates(n)
                 activate(n, F_GATE)
+                activate(n, O_GATE)
             if 0 <= n - 3 < STEPS:
                 tanh_cell(n - 3)
-            if 0 <= n < STEPS:
-                activate(n, O_GATE)
 
             if 1 <= n + 1 < STEPS:
                 multiply(n + 1)

from contextlib import ExitStack

import concourse.mybir as mybir
from concourse.masks import make_identity

F32 = mybir.dt.float32
BF16 = mybir.dt.bfloat16
U32 = mybir.dt.uint32
U8 = mybir.dt.uint8
FP8X4 = mybir.dt.float8_e4m3fn_x4
ACT = mybir.ActivationFunctionType
ALU = mybir.AluOpType

B = 4096
H = 512
P = 128
GATES = 4
I_GATE = 0
G_GATE = 1
F_GATE = 2
O_GATE = 3
ROUND = 512
CHUNKS = H // P
BLOCKS = ROUND // P
STEPS = (B // ROUND) * CHUNKS
HALVES = 2
UNIT = 2
UNIT_COLS = UNIT * P
PAIRS = BLOCKS // UNIT
GATE_UNITS = GATES // UNIT
Z_UNITS = B // (UNIT * P)
FIRST_UNITS = PAIRS
FIRST_CHUNKS = 2
LEAD = 6
LOADS_AHEAD = 4
LAST_LAG = 4

FLOPS = 2 * B * H * GATES * H


def tile_lstmcell_pa_t_kernel(
    tc, inputs, short_term_memory, Wf, b_f, Wi, b_i, Wg, b_g, Wo, b_o, out
):
    nc = tc.nc
    weights = [Wi, Wg, Wf, Wo]
    biases = [b_i, b_g, b_f, b_o]
    functions = [ACT.Sigmoid, ACT.Tanh, ACT.Sigmoid, ACT.Sigmoid]
    gate_names = ["sig_i", "tanh_g", "sig_f", "sig_o"]
    x_view = inputs.rearrange("(r p a t) k -> r a p t k", p=P, a=PAIRS, t=UNIT)
    h_view = short_term_memory.rearrange("(r p a t) k -> r a p t k", p=P, a=PAIRS, t=UNIT)
    out_view = out.rearrange("o (r p s) (m f) -> o r m p s f", p=P, s=BLOCKS, f=P)

    with ExitStack() as ctx:
        keep = ctx.enter_context(tc.tile_pool(name="keep", bufs=1))
        loads = ctx.enter_context(tc.tile_pool(name="loads", bufs=LOADS_AHEAD))
        prep = ctx.enter_context(tc.tile_pool(name="prep", bufs=3))
        w_prep = ctx.enter_context(tc.tile_pool(name="w_prep", bufs=FIRST_CHUNKS * GATE_UNITS))
        gate_pool = ctx.enter_context(tc.tile_pool(name="gates", bufs=LAST_LAG + 1))
        cell_pool = ctx.enter_context(tc.tile_pool(name="cells", bufs=3))
        result_pool = ctx.enter_context(tc.tile_pool(name="results", bufs=4))
        acc_pool = ctx.enter_context(tc.psum_pool(name="acc", bufs=GATES))
        cell_bank = ctx.enter_context(tc.psum_pool(name="cell_bank", bufs=1))
        turn_pool = ctx.enter_context(tc.psum_pool(name="turned", bufs=3))

        ident = keep.tile([P, P], F32, name="ident")
        make_identity(nc, ident[:])

        ctx.enter_context(tc.manual_schedule())

        w_raw = keep.tile([P, CHUNKS, GATES, H], BF16, name="w_raw")
        w_codes = keep.tile([P, CHUNKS, GATES, P], U32, name="w_codes", align_bytes=64)
        w_scales = keep.tile([P, CHUNKS, GATES, P], U8, name="w_scales", align_bytes=64)
        bias_rows = keep.tile([P, P], BF16, name="bias_rows")
        bias_rows_f32 = keep.tile([P, P], F32, name="bias_rows_f32")
        bias = keep.tile([P, GATES * CHUNKS], F32, name="bias")
        zero = keep.tile([P, 1], F32, name="zero")
        half = keep.tile([P, 1], F32, name="half")

        w_turned = {}
        w_grouped = {}
        x_raw = {}
        h_raw = {}
        z_sum = {}
        z_turned = {}
        z_grouped = {}
        z_codes = {}
        z_scales = {}
        acc = {}
        gate = {}
        product = {}
        cell_t = {}
        cell_rows = {}
        sig_o_rows = {}
        cell = {}
        tanh_c = {}


        def turn(source):
            turned = turn_pool.tile([P, UNIT, HALVES, P], F32, name="unit_turned", tag="turned")
            for t in range(UNIT):
                words = source[:, t, :].bitcast(F32)
                for u in range(HALVES):
                    nc.tensor.transpose(turned[:, t, u, :], words[:, u * P : (u + 1) * P], ident[:])
            return turned

        def group(turned, pool, copy):
            grouped = pool.tile([P, UNIT * H], BF16, name="grouped", align_bytes=64)
            copy(
                out=grouped[:].bitcast(F32).rearrange("p (t c u) -> p t c u", t=UNIT, u=HALVES),
                in_=turned[:].rearrange("p t u c -> p t c u"),
            )
            return grouped

        def quantise(grouped, codes, scales):
            nc.vector.quantize_mx(out=codes.bitcast(FP8X4), scales=scales, in_=grouped[:])


        def load_weights(m):
            for g in range(GATES):
                nc.sync.dma_start(out=w_raw[:, m, g, :], in_=weights[g][m * P : (m + 1) * P, :])

        def turn_weights(m):
            w_turned[m] = [
                turn(w_raw[:, m, v * UNIT : (v + 1) * UNIT, :]) for v in range(GATE_UNITS)
            ]

        def group_weights(m, copy):
            w_grouped[m] = [group(turned, w_prep, copy) for turned in w_turned[m]]

        def quantise_weights(m):
            for v in range(GATE_UNITS):
                gates_of_unit = slice(v * UNIT, (v + 1) * UNIT)
                quantise(
                    w_grouped[m][v],
                    w_codes[:, m, gates_of_unit, :].rearrange("p g o -> p (g o)"),
                    w_scales[:, m, gates_of_unit, :].rearrange("p g o -> p (g o)"),
                )

        def load_biases():
            nc.vector.memset(bias_rows[:], 0.0)
            for g in range(GATES):
                nc.scalar.dma_start(
                    out=bias_rows[g * CHUNKS : (g + 1) * CHUNKS, :],
                    in_=biases[g].rearrange("(m c) -> m c", c=P),
                )


        def load_unit(q):
            r, a = divmod(q, PAIRS)
            x_raw[q] = loads.tile([P, UNIT, H], BF16, name="x_raw")
            nc.sync.dma_start(out=x_raw[q][:], in_=x_view[r, a])
            h_raw[q] = loads.tile([P, UNIT, H], BF16, name="h_raw")
            nc.sync.dma_start(out=h_raw[q][:], in_=h_view[r, a])

        def add_z(q):
            z_sum[q] = prep.tile([P, UNIT, H], BF16, name="z_sum")
            nc.vector.tensor_tensor(out=z_sum[q][:], in0=x_raw[q][:], in1=h_raw[q][:], op=ALU.add)
            if q + LOADS_AHEAD < Z_UNITS:
                load_unit(q + LOADS_AHEAD)

        def quantise_z(q):
            r, a = divmod(q, PAIRS)
            if a == 0:
                z_codes[r] = prep.tile([P, ROUND], U32, name="z_codes", align_bytes=64)
                z_scales[r] = prep.tile([P, ROUND], U8, name="z_scales", align_bytes=64)
            columns = slice(a * UNIT_COLS, (a + 1) * UNIT_COLS)
            quantise(z_grouped[q], z_codes[r][:, columns], z_scales[r][:, columns])


        def multiply(n):
            r, m = divmod(n, CHUNKS)
            for g in range(GATES):
                acc[n, g] = acc_pool.tile([P, ROUND], F32, name="acc")
                nc.tensor.matmul_mx(
                    out=acc[n, g][:],
                    lhsT=w_codes[:, m, g, :].bitcast(FP8X4),
                    lhsT_scale=w_scales[:, m, g, :],
                    rhs=z_codes[r][:].bitcast(FP8X4),
                    rhs_scale=z_scales[r][:],
                    start=True,
                    stop=True,
                )

        def activate(n, g):
            gate[n, g] = gate_pool.tile([P, ROUND], F32, name=gate_names[g])
            column = g * CHUNKS + n % CHUNKS
            nc.scalar.activation(
                out=gate[n, g][:],
                in_=acc[n, g][:],
                func=functions[g],
                bias=bias[:, column : column + 1],
                scale=1.0,
            )

        def multiply_gates(n):
            product[n] = cell_pool.tile([P, ROUND], F32, name="product")
            nc.gpsimd.tensor_tensor(
                out=product[n][:], in0=gate[n, I_GATE][:], in1=gate[n, G_GATE][:], op=ALU.mult
            )

        def add_cell(n):
            cell_t[n] = cell_pool.tile([P, ROUND], F32, name="cell_t")
            nc.vector.tensor_tensor(
                out=cell_t[n][:], in0=gate[n, F_GATE][:], in1=product[n][:], op=ALU.add
            )

        def turn_back(rows, source):
            for s in range(BLOCKS):
                nc.tensor.transpose(rows[:, s, :], source[:, s * P : (s + 1) * P], ident[:])

        def turn_cell(n):
            cell_rows[n] = cell_bank.tile([P, BLOCKS, P], F32, name="cell_rows")
            turn_back(cell_rows[n], cell_t[n])

        def turn_sig_o(n):
            sig_o_rows[n] = turn_pool.tile([P, BLOCKS, P], F32, name="sig_o_rows", tag="turned")
            turn_back(sig_o_rows[n], gate[n, O_GATE])

        def copy_cell(n):
            r, m = divmod(n, CHUNKS)
            cell[n] = result_pool.tile([P, BLOCKS, P], F32, name="cell")
            nc.vector.tensor_copy(out=cell[n][:], in_=cell_rows[n][:])
            nc.sync.dma_start(out=out_view[0, r, m], in_=cell[n][:])

        def tanh_cell(n):
            tanh_c[n] = cell_pool.tile([P, BLOCKS, P], F32, name="tanh_c")
            nc.scalar.activation(out=tanh_c[n][:], in_=cell[n][:], func=ACT.Tanh)

        def hidden(n):
            r, m = divmod(n, CHUNKS)
            hidden_rows = result_pool.tile([P, BLOCKS, P], F32, name="hidden_rows")
            nc.vector.tensor_tensor(
                out=hidden_rows[:], in0=tanh_c[n][:], in1=sig_o_rows[n][:], op=ALU.mult
            )
            nc.sync.dma_start(out=out_view[1, r, m], in_=hidden_rows[:])


        load_biases()
        load_unit(0)
        load_unit(1)
        load_weights(0)
        load_weights(1)
        load_unit(2)
        load_weights(2)
        load_unit(3)
        load_weights(3)

        nc.vector.memset(zero[:], 0.0)
        nc.scalar.activation(out=half[:], in_=zero[:], func=ACT.Sigmoid)

        for q in range(FIRST_UNITS):
            add_z(q)
            z_turned[q] = turn(z_sum[q])
        nc.vector.tensor_copy(out=bias_rows_f32[:], in_=bias_rows[:])
        bias_turned = cell_bank.tile([P, BLOCKS, P], F32, name="bias_turned", tag="cell_rows")
        nc.tensor.transpose(bias_turned[:, 0, :], bias_rows_f32[:], ident[:])
        for q in range(FIRST_UNITS):
            z_grouped[q] = group(z_turned[q], prep, nc.vector.tensor_copy)
        nc.vector.tensor_copy(out=bias[:], in_=bias_turned[:, 0, 0 : GATES * CHUNKS])
        for m in range(FIRST_CHUNKS):
            turn_weights(m)
            group_weights(m, nc.scalar.copy)
        for q in range(FIRST_UNITS):
            quantise_z(q)
        quantise_weights(0)
        multiply(0)
        quantise_weights(1)


        for n in range(2 * FIRST_UNITS - LEAD, STEPS + LAST_LAG):
            q, odd = divmod(n + LEAD, 2)

            if 0 <= n - 1 < STEPS:
                add_cell(n - 1)
            if not odd and FIRST_UNITS <= q - 1 < Z_UNITS:
                quantise_z(q - 1)
            if not odd and q < Z_UNITS:
                add_z(q)
            if 0 <= n - 2 < STEPS:
                copy_cell(n - 2)
            if 0 <= n - LAST_LAG < STEPS:
                hidden(n - LAST_LAG)
            if odd and q < Z_UNITS:
                z_grouped[q] = group(z_turned[q], prep, nc.vector.tensor_copy)
            if FIRST_CHUNKS <= n + 2 < CHUNKS:
                group_weights(n + 2, nc.vector.tensor_copy)
                quantise_weights(n + 2)

            if 0 <= n < STEPS:
                activate(n, I_GATE)
                activate(n, G_GATE)
                multiply_gates(n)
                activate(n, F_GATE)
                activate(n, O_GATE)
            if 0 <= n - 3 < STEPS:
                tanh_cell(n - 3)

            if 1 <= n + 1 < STEPS:
                multiply(n + 1)
            if 0 <= n - 1 < STEPS:
                turn_cell(n - 1)
            if 0 <= n - 3 < STEPS:
                turn_sig_o(n - 3)
            if not odd and q < Z_UNITS:
                z_turned[q] = turn(z_sum[q])
            if FIRST_CHUNKS <= n + 3 < CHUNKS:
                turn_weights(n + 3)
